import numpy as np
import ml_dtypes


def mxq(x, axis, fmt="e4m3"):
    dtype, down = {"e4m3": (ml_dtypes.float8_e4m3fn, 7), "e5m2": (ml_dtypes.float8_e5m2, 14)}[fmt]
    v = np.moveaxis(np.asarray(x, np.float32).astype(ml_dtypes.bfloat16).astype(np.float64), axis, -1)
    blocks = v.reshape(v.shape[:-1] + (-1, 32))
    amax = np.abs(blocks).max(-1, keepdims=True)
    byte = np.maximum(np.where(amax > 0, np.frexp(amax)[1] - 1 + 127, 0) - down, 1)
    scale = np.exp2(byte - 127.0)
    codes = (blocks / scale).astype(np.float32).astype(dtype).astype(np.float64)
    return np.moveaxis((codes * scale).reshape(v.shape), -1, axis)


WIDE = False


def mx_kscale(k):
    if not WIDE:
        return np.ones(k)
    levels = np.array([10, -10, 5, -5, 0])
    a = np.random.permutation(np.resize(levels, k // 512 * 4)).reshape(k // 512, 4)
    idx = np.arange(k)
    return np.exp2(a[idx // 512, idx % 128 // 32])


BF16 = ml_dtypes.bfloat16


def bf(x):
    return np.asarray(x, np.float32).astype(BF16)


def f64(x):
    return np.asarray(x).astype(np.float64)


E2M1 = np.array([0.0, 0.5, 1.0, 1.5, 2.0, 3.0, 4.0, 6.0, -0.0, -0.5, -1.0, -1.5, -2.0, -3.0, -4.0, -6.0])


def pack_weight(w, fmt):
    k, n = w.shape
    w = f64(bf(w)).reshape(k // 32, 32, n)
    amax = np.abs(w).max(1)
    if fmt == "e4m3":
        byte = np.frexp(amax)[1] - 1 + 127 - 7
    else:
        mant, ex = np.frexp(amax / 6.0)
        byte = np.where(mant > 0.5, ex, ex - 1) + 127
    byte = np.clip(np.where(amax > 0, byte, 1), 1, 254)
    scaled = (w * np.exp2(127.0 - byte)[:, None, :]).reshape(k, n).astype(np.float32)
    by_word = np.ascontiguousarray(scaled.reshape(k // 512, 128, 4, n).transpose(0, 1, 3, 2))
    if fmt == "e4m3":
        words = by_word.astype(ml_dtypes.float8_e4m3fn).view(np.uint8)
    else:
        c = by_word.astype(ml_dtypes.float4_e2m1fn).view(np.uint8) & 0xF
        words = c[..., 0::2] | (c[..., 1::2] << 4)
    return np.ascontiguousarray(words), np.ascontiguousarray(byte.astype(np.uint8).reshape(k // 512, 16, n))


def unpack_weight(words, scales, fmt):
    g, p, n, _ = words.shape
    if fmt == "e4m3":
        vals = np.ascontiguousarray(words).view(ml_dtypes.float8_e4m3fn).astype(np.float64)
    else:
        nib = np.empty((g, p, n, 4), np.uint8)
        nib[..., 0::2] = words & 0xF
        nib[..., 1::2] = words >> 4
        vals = E2M1[nib]
    vals = vals * np.repeat(np.exp2(scales.astype(np.float64) - 127.0), 8, axis=1)[..., None]
    return vals.transpose(0, 1, 3, 2).reshape(g * 512, n)

def pack4(w):
    words, scales = pack_weight(w, "e2m1")
    return words.reshape(words.shape[0], 128, -1), scales


def unpack4(words, scales):
    return unpack_weight(words.reshape(words.shape[0], 128, -1, 2), scales, "e2m1")


B, F, H, C = 4096, 1024, 128, 10
EPS = 4.0 / 30.0
P_KEEP = 0.95


def setup_inputs():
    s = mx_kscale(F)
    ns = EPS / (6.0 * np.sqrt(H))
    x1 = bf(np.random.standard_normal((B, F)) * s)
    x2 = bf(np.random.standard_normal((B, F)) * s)
    W1_words, W1_scales = pack4(np.random.standard_normal((F, H)) / np.sqrt(F) / s[:, None])
    b1 = bf(np.random.standard_normal(H) * 0.3)
    W2_words, W2_scales = pack4(np.random.standard_normal((F, H)) / np.sqrt(F) / s[:, None])
    b2 = bf(np.random.standard_normal(H) * 0.3)
    noise_std = bf(np.random.laplace(size=(B, H)) * ns)
    rr_uniform = bf(np.random.uniform(size=H))
    return {"x1": x1,
            "x2": x2,
            "W1_words": W1_words,
            "W1_scales": W1_scales,
            "b1": b1,
            "W2_words": W2_words,
            "W2_scales": W2_scales,
            "b2": b2,
            "noise_std": noise_std,
            "rr_uniform": rr_uniform}


def reference(x1, x2, W1_words, W1_scales, b1, W2_words, W2_scales, b2, noise_std, rr_uniform):
    out1 = (mxq(f64(x1), 1, "e4m3") @ unpack4(W1_words, W1_scales)) + f64(b1)
    one_norm = np.sum(np.abs(out1), axis=1)
    sensitivity = np.max(one_norm) - np.min(one_norm)
    noise_mul = sensitivity / EPS
    out1 = out1 + f64(noise_std) * noise_mul
    rr_mask = np.where(f64(rr_uniform) < P_KEEP, 1.0, 0.0)
    out1 = out1 * rr_mask
    out2 = (mxq(f64(x2), 1, "e4m3") @ unpack4(W2_words, W2_scales)) + f64(b2)
    return np.minimum(out1, out2)

@@ -1,0 +1,226 @@
+import concourse.mybir as mybir
+from concourse.masks import make_identity
+
+F32 = mybir.dt.float32
+BF16 = mybir.dt.bfloat16
+U8 = mybir.dt.uint8
+U32 = mybir.dt.uint32
+I32 = mybir.dt.int32
+FP8X4 = mybir.dt.float8_e4m3fn_x4
+FP4X4 = mybir.dt.float4_e2m1fn_x4
+ALU = mybir.AluOpType
+ACT = mybir.ActivationFunctionType
+AXIS = mybir.AxisListType
+
+P = 128
+B, F, H = 4096, 1024, 128
+K_PASS = 4 * P
+PASSES = F // K_PASS
+ROWS = B // P
+CHUNK = 4
+N_CHUNKS = ROWS // CHUNK
+INV_EPS = 7.5
+P_KEEP = 0.95
+
+FLOPS = 2 * 2 * B * F * H
+
+
+def tile_splitnn_pa_t_kernel(
+    tc, x1, x2, W1_words, W1_scales, b1, W2_words, W2_scales, b2, noise_std, rr_uniform, out
+):
+    nc = tc.nc
+    x_views = [x.rearrange("(p r) k -> p r k", r=ROWS) for x in (x1, x2)]
+    noise_view = noise_std.rearrange("(p r) h -> p r h", r=ROWS)
+    out_view = out.rearrange("(p r) h -> p r h", r=ROWS)
+
+    pieces = [(0, first, CHUNK) for first in range(0, ROWS, CHUNK)]
+    pieces += [(1, first, CHUNK) for first in range(0, ROWS - CHUNK, CHUNK)]
+    pieces += [(1, first, CHUNK // 2) for first in range(ROWS - CHUNK, ROWS, CHUNK // 2)]
+    n_pieces = len(pieces)
+
+    with tc.tile_pool(name="const", bufs=1) as const, tc.tile_pool(
+        name="resident", bufs=1
+    ) as resident, tc.tile_pool(name="stage", bufs=3) as stage, tc.psum_pool(
+        name="psum_t", bufs=6
+    ) as psum_t, tc.psum_pool(name="psum_acc", bufs=2) as psum_acc, tc.manual_schedule():
+
+        ident = const.tile([P, P], F32, name="ident")
+        make_identity(nc, ident[:])
+        warm = const.tile([P, 1], F32, name="warm")
+        nc.scalar.activation(out=warm[:], in_=ident[:, 0:1], func=ACT.Abs)
+
+        w_words = [const.tile([P, PASSES, 2 * H], U8, name="w_words%d" % w, align_bytes=64) for w in range(2)]
+        w_planes = [const.tile([P, PASSES, H], U8, name="w_planes%d" % w, align_bytes=64) for w in range(2)]
+        for w in range(2):
+            nc.vector.memset(w_planes[w][:].bitcast(I32), 0)
+
+        def load_weight(w, words, scales):
+            nc.sync.dma_start(
+                out=w_words[w][:].bitcast(I32), in_=words.bitcast(I32).rearrange("g p b -> p g b")
+            )
+            scale_rows = scales.bitcast(I32).rearrange("g q n -> q g n")
+            for quad in range(4):
+                nc.sync.dma_start(
+                    out=w_planes[w][32 * quad : 32 * quad + 4].bitcast(I32),
+                    in_=scale_rows[4 * quad : 4 * quad + 4],
+                )
+
+        def load_x(client, first, n_rows, rows_per_load):
+            row_words = []
+            for start in range(first, first + n_rows, rows_per_load):
+                x_sb = resident.tile([P, rows_per_load, F], BF16, name="x%d_%d" % (client, start))
+                nc.sync.dma_start(out=x_sb[:], in_=x_views[client][:, start : start + rows_per_load, :])
+                words = x_sb[:].bitcast(F32)
+                for i in range(rows_per_load):
+                    row_words.append(words[:, i, :])
+            return row_words
+
+        vec_bf = {}
+        for name, vec in (("b1", b1), ("rr", rr_uniform), ("b2", b2)):
+            vec_bf[name] = const.tile([P, H], BF16, name="%s_bf" % name)
+            nc.scalar.dma_start(out=vec_bf[name][:], in_=vec.partition_broadcast(P))
+
+        x_rows = []
+        noise = []
+        for index, (client, first, n_rows) in enumerate(pieces):
+            if index == N_CHUNKS:
+                load_weight(1, W2_words, W2_scales)
+            x_rows.append(load_x(client, first, n_rows, 1 if index == 0 else n_rows))
+            if index == 0:
+                load_weight(0, W1_words, W1_scales)
+            if client == 0:
+                noise_sb = resident.tile([P, CHUNK, H], BF16, name="noise%d" % index)
+                nc.sync.dma_start(out=noise_sb[:], in_=noise_view[:, first : first + CHUNK, :])
+                noise.append(noise_sb)
+
+        def transpose_piece(rows):
+            banks = []
+            for row in rows:
+                xt = psum_t.tile([P, PASSES, 2, P], F32, name="xt")
+                for g in range(PASSES):
+                    for u in range(2):
+                        nc.tensor.transpose(xt[:, g, u, :], row[:, 256 * g + u : 256 * (g + 1) : 2], ident[:])
+                banks.append(xt)
+            return banks
+
+        def regroup_piece(banks):
+            n_rows = len(banks)
+            grouped = stage.tile([P, n_rows * PASSES * P * 4], BF16, name="grouped", align_bytes=64)
+            words = grouped[:].bitcast(F32).rearrange("p (j g t u) -> p j g t u", j=n_rows, g=PASSES, u=2)
+            for j in range(n_rows):
+                nc.scalar.copy(out=words[:, j], in_=banks[j][:].rearrange("p g u t -> p g t u"))
+            return grouped
+
+        def quantise_piece(grouped, n_rows):
+            codes = stage.tile([P, n_rows * PASSES * P], U32, name="codes", align_bytes=64)
+            scales = stage.tile([P, n_rows * PASSES * P], U8, name="scales", align_bytes=64)
+            nc.vector.quantize_mx(out=codes[:].bitcast(FP8X4), scales=scales[:], in_=grouped[:])
+            return codes, scales
+
+        def multiply_piece(client, n_rows, codes, scales):
+            acc = psum_acc.tile([P, n_rows, H], F32, name="acc")
+            for j in range(n_rows):
+                for g in range(PASSES):
+                    cols = slice((j * PASSES + g) * P, (j * PASSES + g + 1) * P)
+                    nc.tensor.matmul_mx(
+                        out=acc[:, j, :],
+                        lhsT=codes[:, cols].bitcast(FP8X4),
+                        lhsT_scale=scales[:, cols],
+                        rhs=w_words[client][:, g, :].bitcast(FP4X4),
+                        rhs_scale=w_planes[client][:, g, :],
+                        start=(g == 0),
+                        stop=(g == PASSES - 1),
+                    )
+            return acc
+
+        def over_rows(vec, n_rows):
+            return vec[:].unsqueeze(1).to_broadcast([P, n_rows, H])
+
+        b1_f = const.tile([P, H], F32, name="b1_f")
+        b2_f = const.tile([P, H], F32, name="b2_f")
+        keep_f = const.tile([P, H], F32, name="keep_f")
+        keep_bf = const.tile([P, H], BF16, name="keep_bf")
+        norms = const.tile([P, ROWS], F32, name="norms")
+        extremes = const.tile([P, 2], F32, name="extremes")
+        spread = const.tile([P, 2, P], F32, name="spread")
+        tops = const.tile([P, 2], F32, name="tops")
+        noise_mul = const.tile([P, 1], F32, name="noise_mul")
+
+        def row_norms(a_sb, first):
+            absolute = stage.tile([P, CHUNK, H], BF16, name="absolute")
+            for j in range(CHUNK):
+                nc.scalar.activation(
+                    out=absolute[:, j, :], in_=a_sb[:, j, :], func=ACT.Abs,
+                    accum_out=norms[:, first + j : first + j + 1],
+                )
+
+        def add_noise(chunk):
+            flat_c = c_tiles[chunk][:].rearrange("p j h -> p (j h)")
+            nc.vector.scalar_tensor_tensor(
+                out=flat_c, in0=noise[chunk][:].rearrange("p j h -> p (j h)"),
+                scalar=noise_mul[:, 0:1], in1=flat_c, op0=ALU.mult, op1=ALU.add,
+            )
+
+        a_tiles = {}
+        c_tiles = []
+        quantised = {}
+        for step in range(n_pieces + 1):
+            if step < n_pieces:
+                grouped = regroup_piece(transpose_piece(x_rows[step]))
+            if 2 <= step <= N_CHUNKS:
+                row_norms(a_tiles[step - 2], pieces[step - 2][1])
+            if step >= 1:
+                client, first, n_rows = pieces[step - 1]
+                codes, scales = quantised[step - 1]
+                acc = multiply_piece(client, n_rows, codes, scales)
+                if client == 0:
+                    a_sb = stage.tile([P, CHUNK, H], F32, name="a_sb")
+                    a_tiles[step - 1] = a_sb
+                    nc.vector.tensor_tensor(out=a_sb[:], in0=acc[:], in1=over_rows(b1_f, n_rows), op=ALU.add)
+                else:
+                    d_sb = stage.tile([P, n_rows, H], F32, name="d_sb")
+                    nc.vector.tensor_tensor(out=d_sb[:], in0=acc[:], in1=over_rows(b2_f, n_rows), op=ALU.add)
+            if step == N_CHUNKS:
+                row_norms(a_tiles[step - 1], pieces[step - 1][1])
+            if step == N_CHUNKS + 1:
+                spread_t = psum_acc.tile([P, 2, P], F32, name="spread_t", tag="acc")
+                for i in range(2):
+                    nc.tensor.transpose(spread_t[:, i, :], spread[:, i, :], ident[:])
+            if step < n_pieces:
+                quantised[step] = quantise_piece(grouped, pieces[step][2])
+            if step == 0:
+                nc.vector.tensor_copy(out=b1_f[:], in_=vec_bf["b1"][:])
+                nc.vector.tensor_copy(out=b2_f[:], in_=vec_bf["b2"][:])
+                nc.vector.tensor_single_scalar(out=keep_f[:], in_=vec_bf["rr"][:], scalar=P_KEEP, op=ALU.is_lt)
+                nc.vector.tensor_single_scalar(out=keep_bf[:], in_=vec_bf["rr"][:], scalar=P_KEEP, op=ALU.is_lt)
+            if step >= 1 and client == 0:
+                chunk = first // CHUNK
+                nc.vector.tensor_tensor(
+                    out=noise[chunk][:], in0=noise[chunk][:], in1=over_rows(keep_bf, CHUNK), op=ALU.mult
+                )
+                c_sb = resident.tile([P, CHUNK, H], F32, name="c%d" % chunk)
+                c_tiles.append(c_sb)
+                nc.vector.tensor_tensor(out=c_sb[:], in0=a_sb[:], in1=over_rows(keep_f, CHUNK), op=ALU.mult)
+                if chunk == N_CHUNKS - 1:
+                    nc.vector.tensor_reduce(out=extremes[:, 0:1], in_=norms[:], axis=AXIS.X, op=ALU.max)
+                    nc.vector.tensor_reduce(out=extremes[:, 1:2], in_=norms[:], axis=AXIS.X, op=ALU.min)
+                    nc.vector.tensor_copy(out=spread[:, 0, :], in_=extremes[:, 0:1].to_broadcast([P, P]))
+                    nc.vector.tensor_scalar_mul(
+                        out=spread[:, 1, :], in0=extremes[:, 1:2].to_broadcast([P, P]), scalar1=-1.0
+                    )
+            if step >= 1 and client == 1:
+                if first == 0:
+                    nc.vector.tensor_reduce(out=tops[:], in_=spread_t[:], axis=AXIS.X, op=ALU.max)
+                    nc.vector.tensor_scalar(
+                        out=noise_mul[:], in0=tops[:, 0:1], scalar1=tops[:, 1:2], scalar2=INV_EPS,
+                        op0=ALU.add, op1=ALU.mult,
+                    )
+                    add_noise(0)
+                if first % CHUNK == 0 and first + CHUNK < ROWS:
+                    add_noise(first // CHUNK + 1)
+                offset = first % CHUNK
+                nc.vector.tensor_tensor(
+                    out=d_sb[:], in0=d_sb[:], in1=c_tiles[first // CHUNK][:, offset : offset + n_rows, :],
+                    op=ALU.min,
+                )
+                nc.sync.dma_start(out=out_view[:, first : first + n_rows, :], in_=d_sb[:])

@@ -44,6 +44,14 @@ def tile_splitnn_pa_t_kernel(
         name="psum_t", bufs=6
     ) as psum_t, tc.psum_pool(name="psum_acc", bufs=2) as psum_acc, tc.manual_schedule():
 
+        vec_rows = const.tile([P, 3 * H], BF16, name="vec_rows")
+        nc.vector.memset(vec_rows[:], 0.0)
+        ones_bf = const.tile([P, P], BF16, name="ones_bf")
+        nc.vector.memset(ones_bf[:], 1.0)
+        for i, vec in enumerate((b1, rr_uniform, b2)):
+            nc.scalar.dma_start(
+                out=vec_rows[0:1, i * H : (i + 1) * H], in_=vec.rearrange("(o h) -> o h", o=1)
+            )
         ident = const.tile([P, P], F32, name="ident")
         make_identity(nc, ident[:])
         warm = const.tile([P, 1], F32, name="warm")
@@ -75,10 +83,6 @@ def tile_splitnn_pa_t_kernel(
                     row_words.append(words[:, i, :])
             return row_words
 
-        vec_bf = {}
-        for name, vec in (("b1", b1), ("rr", rr_uniform), ("b2", b2)):
-            vec_bf[name] = const.tile([P, H], BF16, name="%s_bf" % name)
-            nc.scalar.dma_start(out=vec_bf[name][:], in_=vec.partition_broadcast(P))
 
         x_rows = []
         noise = []
@@ -167,6 +171,13 @@ def tile_splitnn_pa_t_kernel(
         for step in range(n_pieces + 1):
             if step < n_pieces:
                 grouped = regroup_piece(transpose_piece(x_rows[step]))
+            if step == 0:
+                vec_all = psum_acc.tile([P, 3 * H], F32, name="vec_all", tag="acc")
+                nc.tensor.matmul(out=vec_all[:], lhsT=ones_bf[:], rhs=vec_rows[:], start=True, stop=True)
+                nc.vector.tensor_copy(out=b1_f[:], in_=vec_all[:, 0:H])
+                nc.vector.tensor_copy(out=b2_f[:], in_=vec_all[:, 2 * H : 3 * H])
+                nc.vector.tensor_single_scalar(out=keep_f[:], in_=vec_all[:, H : 2 * H], scalar=P_KEEP, op=ALU.is_lt)
+                nc.vector.tensor_single_scalar(out=keep_bf[:], in_=vec_all[:, H : 2 * H], scalar=P_KEEP, op=ALU.is_lt)
             if 2 <= step <= N_CHUNKS:
                 row_norms(a_tiles[step - 2], pieces[step - 2][1])
             if step >= 1:
@@ -188,11 +199,6 @@ def tile_splitnn_pa_t_kernel(
                     nc.tensor.transpose(spread_t[:, i, :], spread[:, i, :], ident[:])
             if step < n_pieces:
                 quantised[step] = quantise_piece(grouped, pieces[step][2])
-            if step == 0:
-                nc.vector.tensor_copy(out=b1_f[:], in_=vec_bf["b1"][:])
-                nc.vector.tensor_copy(out=b2_f[:], in_=vec_bf["b2"][:])
-                nc.vector.tensor_single_scalar(out=keep_f[:], in_=vec_bf["rr"][:], scalar=P_KEEP, op=ALU.is_lt)
-                nc.vector.tensor_single_scalar(out=keep_bf[:], in_=vec_bf["rr"][:], scalar=P_KEEP, op=ALU.is_lt)
             if step >= 1 and client == 0:
                 chunk = first // CHUNK
                 nc.vector.tensor_tensor(

@@ -19,6 +19,7 @@ PASSES = F // K_PASS
 ROWS = B // P
 CHUNK = 4
 N_CHUNKS = ROWS // CHUNK
+RUN = 4
 INV_EPS = 7.5
 P_KEEP = 0.95
 
@@ -97,9 +98,9 @@ def tile_splitnn_pa_t_kernel(
                 nc.sync.dma_start(out=noise_sb[:], in_=noise_view[:, first : first + CHUNK, :])
                 noise.append(noise_sb)
 
-        def transpose_piece(rows):
+        def transpose_run(rows):
             banks = []
-            for row in rows:
+            for i, row in enumerate(rows):
                 xt = psum_t.tile([P, PASSES, 2, P], F32, name="xt")
                 for g in range(PASSES):
                     for u in range(2):
@@ -107,7 +108,7 @@ def tile_splitnn_pa_t_kernel(
                 banks.append(xt)
             return banks
 
-        def regroup_piece(banks):
+        def regroup_run(banks):
             n_rows = len(banks)
             grouped = stage.tile([P, n_rows * PASSES * P * 4], BF16, name="grouped", align_bytes=64)
             words = grouped[:].bitcast(F32).rearrange("p (j g t u) -> p j g t u", j=n_rows, g=PASSES, u=2)
@@ -115,19 +116,18 @@ def tile_splitnn_pa_t_kernel(
                 nc.scalar.copy(out=words[:, j], in_=banks[j][:].rearrange("p g u t -> p g t u"))
             return grouped
 
-        def quantise_piece(grouped, n_rows):
+        def quantise_run(grouped, n_rows):
             codes = stage.tile([P, n_rows * PASSES * P], U32, name="codes", align_bytes=64)
             scales = stage.tile([P, n_rows * PASSES * P], U8, name="scales", align_bytes=64)
             nc.vector.quantize_mx(out=codes[:].bitcast(FP8X4), scales=scales[:], in_=grouped[:])
             return codes, scales
 
-        def multiply_piece(client, n_rows, codes, scales):
-            acc = psum_acc.tile([P, n_rows, H], F32, name="acc")
+        def multiply_run(client, acc, start, n_rows, codes, scales):
             for j in range(n_rows):
                 for g in range(PASSES):
                     cols = slice((j * PASSES + g) * P, (j * PASSES + g + 1) * P)
                     nc.tensor.matmul_mx(
-                        out=acc[:, j, :],
+                        out=acc[:, start + j, :],
                         lhsT=codes[:, cols].bitcast(FP8X4),
                         lhsT_scale=scales[:, cols],
                         rhs=w_words[client][:, g, :].bitcast(FP4X4),
@@ -135,7 +135,6 @@ def tile_splitnn_pa_t_kernel(
                         start=(g == 0),
                         stop=(g == PASSES - 1),
                     )
-            return acc
 
         def over_rows(vec, n_rows):
             return vec[:].unsqueeze(1).to_broadcast([P, n_rows, H])
@@ -165,68 +164,90 @@ def tile_splitnn_pa_t_kernel(
                 scalar=noise_mul[:, 0:1], in1=flat_c, op0=ALU.mult, op1=ALU.add,
             )
 
-        a_tiles = {}
         c_tiles = []
+
+        def mask_client0(chunk, a_sb):
+            nc.vector.tensor_tensor(
+                out=noise[chunk][:], in0=noise[chunk][:], in1=over_rows(keep_bf, CHUNK), op=ALU.mult
+            )
+            c_sb = resident.tile([P, CHUNK, H], F32, name="c%d" % chunk)
+            c_tiles.append(c_sb)
+            nc.vector.tensor_tensor(out=c_sb[:], in0=a_sb[:], in1=over_rows(keep_f, CHUNK), op=ALU.mult)
+
+        def finish_client0(index, acc):
+            first = pieces[index][1]
+            chunk = first // CHUNK
+            a_sb = stage.tile([P, CHUNK, H], F32, name="a_sb")
+            nc.vector.tensor_tensor(out=a_sb[:], in0=acc[:], in1=over_rows(b1_f, CHUNK), op=ALU.add)
+            if chunk < N_CHUNKS - 1:
+                norms_due.append((a_sb, first))
+            else:
+                row_norms(a_sb, first)
+            mask_client0(chunk, a_sb)
+            if chunk == N_CHUNKS - 1:
+                nc.vector.tensor_reduce(out=extremes[:, 0:1], in_=norms[:], axis=AXIS.X, op=ALU.max)
+                nc.vector.tensor_reduce(out=extremes[:, 1:2], in_=norms[:], axis=AXIS.X, op=ALU.min)
+                nc.vector.tensor_copy(out=spread[:, 0, :], in_=extremes[:, 0:1].to_broadcast([P, P]))
+                nc.vector.tensor_scalar_mul(
+                    out=spread[:, 1, :], in0=extremes[:, 1:2].to_broadcast([P, P]), scalar1=-1.0
+                )
+
+        def finish_client1(index, acc):
+            client, first, n_rows = pieces[index]
+            d_sb = stage.tile([P, n_rows, H], F32, name="d_sb")
+            nc.vector.tensor_tensor(out=d_sb[:], in0=acc[:], in1=over_rows(b2_f, n_rows), op=ALU.add)
+            if first == 0:
+                spread_t = psum_acc.tile([P, 2, P], F32, name="spread_t", tag="acc")
+                for i in range(2):
+                    nc.tensor.transpose(spread_t[:, i, :], spread[:, i, :], ident[:])
+                nc.vector.tensor_reduce(out=tops[:], in_=spread_t[:], axis=AXIS.X, op=ALU.max)
+                nc.vector.tensor_scalar(
+                    out=noise_mul[:], in0=tops[:, 0:1], scalar1=tops[:, 1:2], scalar2=INV_EPS,
+                    op0=ALU.add, op1=ALU.mult,
+                )
+                add_noise(0)
+            if first % CHUNK == 0 and first + CHUNK < ROWS:
+                add_noise(first // CHUNK + 1)
+            offset = first % CHUNK
+            nc.vector.tensor_tensor(
+                out=d_sb[:], in0=d_sb[:], in1=c_tiles[first // CHUNK][:, offset : offset + n_rows, :],
+                op=ALU.min,
+            )
+            nc.sync.dma_start(out=out_view[:, first : first + n_rows, :], in_=d_sb[:])
+
+        runs = []
+        for index, piece in enumerate(pieces):
+            for start in range(0, piece[2], RUN):
+                runs.append((index, start, min(RUN, piece[2] - start)))
+        n_runs = len(runs)
+
+        norms_due = []
         quantised = {}
-        for step in range(n_pieces + 1):
-            if step < n_pieces:
-                grouped = regroup_piece(transpose_piece(x_rows[step]))
-            if step == 0:
+        accs = {}
+        for step in range(n_runs + 1):
+            if step < n_runs:
+                index, start, n_rows = runs[step]
+                grouped = regroup_run(transpose_run(x_rows[index][start : start + n_rows]))
+                quantised[step] = quantise_run(grouped, n_rows)
+            if step == 1:
                 vec_all = psum_acc.tile([P, 3 * H], F32, name="vec_all", tag="acc")
                 nc.tensor.matmul(out=vec_all[:], lhsT=ones_bf[:], rhs=vec_rows[:], start=True, stop=True)
                 nc.vector.tensor_copy(out=b1_f[:], in_=vec_all[:, 0:H])
                 nc.vector.tensor_copy(out=b2_f[:], in_=vec_all[:, 2 * H : 3 * H])
                 nc.vector.tensor_single_scalar(out=keep_f[:], in_=vec_all[:, H : 2 * H], scalar=P_KEEP, op=ALU.is_lt)
                 nc.vector.tensor_single_scalar(out=keep_bf[:], in_=vec_all[:, H : 2 * H], scalar=P_KEEP, op=ALU.is_lt)
-            if 2 <= step <= N_CHUNKS:
-                row_norms(a_tiles[step - 2], pieces[step - 2][1])
+            for a_sb, first in norms_due:
+                row_norms(a_sb, first)
+            norms_due.clear()
             if step >= 1:
-                client, first, n_rows = pieces[step - 1]
+                index, start, n_rows = runs[step - 1]
+                client, first, piece_rows = pieces[index]
+                if start == 0:
+                    accs[index] = psum_acc.tile([P, piece_rows, H], F32, name="acc")
                 codes, scales = quantised[step - 1]
-                acc = multiply_piece(client, n_rows, codes, scales)
-                if client == 0:
-                    a_sb = stage.tile([P, CHUNK, H], F32, name="a_sb")
-                    a_tiles[step - 1] = a_sb
-                    nc.vector.tensor_tensor(out=a_sb[:], in0=acc[:], in1=over_rows(b1_f, n_rows), op=ALU.add)
-                else:
-                    d_sb = stage.tile([P, n_rows, H], F32, name="d_sb")
-                    nc.vector.tensor_tensor(out=d_sb[:], in0=acc[:], in1=over_rows(b2_f, n_rows), op=ALU.add)
-            if step == N_CHUNKS:
-                row_norms(a_tiles[step - 1], pieces[step - 1][1])
-            if step == N_CHUNKS + 1:
-                spread_t = psum_acc.tile([P, 2, P], F32, name="spread_t", tag="acc")
-                for i in range(2):
-                    nc.tensor.transpose(spread_t[:, i, :], spread[:, i, :], ident[:])
-            if step < n_pieces:
-                quantised[step] = quantise_piece(grouped, pieces[step][2])
-            if step >= 1 and client == 0:
-                chunk = first // CHUNK
-                nc.vector.tensor_tensor(
-                    out=noise[chunk][:], in0=noise[chunk][:], in1=over_rows(keep_bf, CHUNK), op=ALU.mult
-                )
-                c_sb = resident.tile([P, CHUNK, H], F32, name="c%d" % chunk)
-                c_tiles.append(c_sb)
-                nc.vector.tensor_tensor(out=c_sb[:], in0=a_sb[:], in1=over_rows(keep_f, CHUNK), op=ALU.mult)
-                if chunk == N_CHUNKS - 1:
-                    nc.vector.tensor_reduce(out=extremes[:, 0:1], in_=norms[:], axis=AXIS.X, op=ALU.max)
-                    nc.vector.tensor_reduce(out=extremes[:, 1:2], in_=norms[:], axis=AXIS.X, op=ALU.min)
-                    nc.vector.tensor_copy(out=spread[:, 0, :], in_=extremes[:, 0:1].to_broadcast([P, P]))
-                    nc.vector.tensor_scalar_mul(
-                        out=spread[:, 1, :], in0=extremes[:, 1:2].to_broadcast([P, P]), scalar1=-1.0
-                    )
-            if step >= 1 and client == 1:
-                if first == 0:
-                    nc.vector.tensor_reduce(out=tops[:], in_=spread_t[:], axis=AXIS.X, op=ALU.max)
-                    nc.vector.tensor_scalar(
-                        out=noise_mul[:], in0=tops[:, 0:1], scalar1=tops[:, 1:2], scalar2=INV_EPS,
-                        op0=ALU.add, op1=ALU.mult,
-                    )
-                    add_noise(0)
-                if first % CHUNK == 0 and first + CHUNK < ROWS:
-                    add_noise(first // CHUNK + 1)
-                offset = first % CHUNK
-                nc.vector.tensor_tensor(
-                    out=d_sb[:], in0=d_sb[:], in1=c_tiles[first // CHUNK][:, offset : offset + n_rows, :],
-                    op=ALU.min,
-                )
-                nc.sync.dma_start(out=out_view[:, first : first + n_rows, :], in_=d_sb[:])
+                multiply_run(client, accs[index], start, n_rows, codes, scales)
+                if start + n_rows == piece_rows:
+                    if client == 0:
+                        finish_client0(index, accs[index])
+                    else:
+                        finish_client1(index, accs[index])

@@ -19,6 +19,7 @@ PASSES = F // K_PASS
 ROWS = B // P
 CHUNK = 4
 N_CHUNKS = ROWS // CHUNK
+Q_LAG, M_LAG, E_LAG = 1, 2, 3
 RUN = 4
 INV_EPS = 7.5
 P_KEEP = 0.95
@@ -41,7 +42,7 @@ def tile_splitnn_pa_t_kernel(
 
     with tc.tile_pool(name="const", bufs=1) as const, tc.tile_pool(
         name="resident", bufs=1
-    ) as resident, tc.tile_pool(name="stage", bufs=3) as stage, tc.psum_pool(
+    ) as resident, tc.tile_pool(name="stage", bufs=4) as stage, tc.psum_pool(
         name="psum_t", bufs=6
     ) as psum_t, tc.psum_pool(name="psum_acc", bufs=2) as psum_acc, tc.manual_schedule():
 
@@ -197,10 +198,7 @@ def tile_splitnn_pa_t_kernel(
             d_sb = stage.tile([P, n_rows, H], F32, name="d_sb")
             nc.vector.tensor_tensor(out=d_sb[:], in0=acc[:], in1=over_rows(b2_f, n_rows), op=ALU.add)
             if first == 0:
-                spread_t = psum_acc.tile([P, 2, P], F32, name="spread_t", tag="acc")
-                for i in range(2):
-                    nc.tensor.transpose(spread_t[:, i, :], spread[:, i, :], ident[:])
-                nc.vector.tensor_reduce(out=tops[:], in_=spread_t[:], axis=AXIS.X, op=ALU.max)
+                nc.vector.tensor_reduce(out=tops[:], in_=spread_ts[0][:], axis=AXIS.X, op=ALU.max)
                 nc.vector.tensor_scalar(
                     out=noise_mul[:], in0=tops[:, 0:1], scalar1=tops[:, 1:2], scalar2=INV_EPS,
                     op0=ALU.add, op1=ALU.mult,
@@ -222,30 +220,45 @@ def tile_splitnn_pa_t_kernel(
         n_runs = len(runs)
 
         norms_due = []
+        grouped_of = {}
         quantised = {}
         accs = {}
-        for step in range(n_runs + 1):
+        spread_ts = []
+        last0 = max(i for i in range(n_runs) if pieces[runs[i][0]][0] == 0)
+        for step in range(n_runs + E_LAG):
+            if step == last0 + E_LAG + 1:
+                spread_t = psum_t.tile([P, 2, P], F32, name="spread_t", tag="xt")
+                spread_ts.append(spread_t)
+                for i in range(2):
+                    nc.tensor.transpose(spread_t[:, i, :], spread[:, i, :], ident[:])
             if step < n_runs:
                 index, start, n_rows = runs[step]
-                grouped = regroup_run(transpose_run(x_rows[index][start : start + n_rows]))
-                quantised[step] = quantise_run(grouped, n_rows)
+                grouped_of[step] = regroup_run(transpose_run(x_rows[index][start : start + n_rows]))
+            for a_sb, first in norms_due:
+                row_norms(a_sb, first)
+            norms_due.clear()
+            q = step - Q_LAG
+            if 0 <= q < n_runs:
+                quantised[q] = quantise_run(grouped_of[q], runs[q][2])
             if step == 1:
-                vec_all = psum_acc.tile([P, 3 * H], F32, name="vec_all", tag="acc")
+                vec_all = psum_t.tile([P, 3 * H], F32, name="vec_all", tag="xt")
                 nc.tensor.matmul(out=vec_all[:], lhsT=ones_bf[:], rhs=vec_rows[:], start=True, stop=True)
                 nc.vector.tensor_copy(out=b1_f[:], in_=vec_all[:, 0:H])
                 nc.vector.tensor_copy(out=b2_f[:], in_=vec_all[:, 2 * H : 3 * H])
                 nc.vector.tensor_single_scalar(out=keep_f[:], in_=vec_all[:, H : 2 * H], scalar=P_KEEP, op=ALU.is_lt)
                 nc.vector.tensor_single_scalar(out=keep_bf[:], in_=vec_all[:, H : 2 * H], scalar=P_KEEP, op=ALU.is_lt)
-            for a_sb, first in norms_due:
-                row_norms(a_sb, first)
-            norms_due.clear()
-            if step >= 1:
-                index, start, n_rows = runs[step - 1]
+            m = step - M_LAG
+            if 0 <= m < n_runs:
+                index, start, n_rows = runs[m]
                 client, first, piece_rows = pieces[index]
                 if start == 0:
                     accs[index] = psum_acc.tile([P, piece_rows, H], F32, name="acc")
-                codes, scales = quantised[step - 1]
+                codes, scales = quantised[m]
                 multiply_run(client, accs[index], start, n_rows, codes, scales)
+            e = step - E_LAG
+            if 0 <= e < n_runs:
+                index, start, n_rows = runs[e]
+                client, first, piece_rows = pieces[index]
                 if start + n_rows == piece_rows:
                     if client == 0:
                         finish_client0(index, accs[index])

@@ -20,6 +20,8 @@ ROWS = B // P
 CHUNK = 4
 N_CHUNKS = ROWS // CHUNK
 Q_LAG, M_LAG, E_LAG = 1, 2, 3
+AHEAD = 4
+BY_ROW = 2
 RUN = 4
 INV_EPS = 7.5
 P_KEEP = 0.95
@@ -50,10 +52,13 @@ def tile_splitnn_pa_t_kernel(
         nc.vector.memset(vec_rows[:], 0.0)
         ones_bf = const.tile([P, P], BF16, name="ones_bf")
         nc.vector.memset(ones_bf[:], 1.0)
-        for i, vec in enumerate((b1, rr_uniform, b2)):
-            nc.scalar.dma_start(
-                out=vec_rows[0:1, i * H : (i + 1) * H], in_=vec.rearrange("(o h) -> o h", o=1)
-            )
+
+        def load_vectors():
+            for i, vec in enumerate((b1, rr_uniform, b2)):
+                nc.scalar.dma_start(
+                    out=vec_rows[0:1, i * H : (i + 1) * H], in_=vec.rearrange("(o h) -> o h", o=1)
+                )
+
         ident = const.tile([P, P], F32, name="ident")
         make_identity(nc, ident[:])
         warm = const.tile([P, 1], F32, name="warm")
@@ -85,19 +90,24 @@ def tile_splitnn_pa_t_kernel(
                     row_words.append(words[:, i, :])
             return row_words
 
-
         x_rows = []
         noise = []
-        for index, (client, first, n_rows) in enumerate(pieces):
-            if index == N_CHUNKS:
-                load_weight(1, W2_words, W2_scales)
-            x_rows.append(load_x(client, first, n_rows, 1 if index == 0 else n_rows))
-            if index == 0:
+
+        def load_piece(index):
+            client, first, n_rows = pieces[index]
+            x_rows.append(load_x(client, first, n_rows, 1 if index < BY_ROW else n_rows))
+            if index == 1:
                 load_weight(0, W1_words, W1_scales)
-            if client == 0:
-                noise_sb = resident.tile([P, CHUNK, H], BF16, name="noise%d" % index)
-                nc.sync.dma_start(out=noise_sb[:], in_=noise_view[:, first : first + CHUNK, :])
+            if index == 4:
+                load_weight(1, W2_words, W2_scales)
+            late = index - 1
+            if 0 <= late < N_CHUNKS:
+                noise_sb = resident.tile([P, CHUNK, H], BF16, name="noise%d" % late)
+                nc.sync.dma_start(out=noise_sb[:], in_=noise_view[:, late * CHUNK : (late + 1) * CHUNK, :])
                 noise.append(noise_sb)
+
+        for index in range(AHEAD):
+            load_piece(index)
 
         def transpose_run(rows):
             banks = []
@@ -180,18 +190,16 @@ def tile_splitnn_pa_t_kernel(
             chunk = first // CHUNK
             a_sb = stage.tile([P, CHUNK, H], F32, name="a_sb")
             nc.vector.tensor_tensor(out=a_sb[:], in0=acc[:], in1=over_rows(b1_f, CHUNK), op=ALU.add)
-            if chunk < N_CHUNKS - 1:
-                norms_due.append((a_sb, first))
-            else:
-                row_norms(a_sb, first)
+            norms_due.append((a_sb, first))
             mask_client0(chunk, a_sb)
-            if chunk == N_CHUNKS - 1:
-                nc.vector.tensor_reduce(out=extremes[:, 0:1], in_=norms[:], axis=AXIS.X, op=ALU.max)
-                nc.vector.tensor_reduce(out=extremes[:, 1:2], in_=norms[:], axis=AXIS.X, op=ALU.min)
-                nc.vector.tensor_copy(out=spread[:, 0, :], in_=extremes[:, 0:1].to_broadcast([P, P]))
-                nc.vector.tensor_scalar_mul(
-                    out=spread[:, 1, :], in0=extremes[:, 1:2].to_broadcast([P, P]), scalar1=-1.0
-                )
+
+        def find_extremes():
+            nc.vector.tensor_reduce(out=extremes[:, 0:1], in_=norms[:], axis=AXIS.X, op=ALU.max)
+            nc.vector.tensor_reduce(out=extremes[:, 1:2], in_=norms[:], axis=AXIS.X, op=ALU.min)
+            nc.vector.tensor_copy(out=spread[:, 0, :], in_=extremes[:, 0:1].to_broadcast([P, P]))
+            nc.vector.tensor_scalar_mul(
+                out=spread[:, 1, :], in0=extremes[:, 1:2].to_broadcast([P, P]), scalar1=-1.0
+            )
 
         def finish_client1(index, acc):
             client, first, n_rows = pieces[index]
@@ -226,27 +234,25 @@ def tile_splitnn_pa_t_kernel(
         spread_ts = []
         last0 = max(i for i in range(n_runs) if pieces[runs[i][0]][0] == 0)
         for step in range(n_runs + E_LAG):
+            for a_sb, first in norms_due:
+                row_norms(a_sb, first)
+            norms_due.clear()
+            if step + AHEAD < n_pieces:
+                load_piece(step + AHEAD)
+            if step < n_runs:
+                index, start, n_rows = runs[step]
+                grouped_of[step] = regroup_run(transpose_run(x_rows[index][start : start + n_rows]))
+            if step == 0:
+                load_vectors()
+            q = step - Q_LAG
+            if 0 <= q < n_runs:
+                quantised[q] = quantise_run(grouped_of[q], runs[q][2])
             if step == last0 + E_LAG + 1:
+                find_extremes()
                 spread_t = psum_t.tile([P, 2, P], F32, name="spread_t", tag="xt")
                 spread_ts.append(spread_t)
                 for i in range(2):
                     nc.tensor.transpose(spread_t[:, i, :], spread[:, i, :], ident[:])
-            if step < n_runs:
-                index, start, n_rows = runs[step]
-                grouped_of[step] = regroup_run(transpose_run(x_rows[index][start : start + n_rows]))
-            for a_sb, first in norms_due:
-                row_norms(a_sb, first)
-            norms_due.clear()
-            q = step - Q_LAG
-            if 0 <= q < n_runs:
-                quantised[q] = quantise_run(grouped_of[q], runs[q][2])
-            if step == 1:
-                vec_all = psum_t.tile([P, 3 * H], F32, name="vec_all", tag="xt")
-                nc.tensor.matmul(out=vec_all[:], lhsT=ones_bf[:], rhs=vec_rows[:], start=True, stop=True)
-                nc.vector.tensor_copy(out=b1_f[:], in_=vec_all[:, 0:H])
-                nc.vector.tensor_copy(out=b2_f[:], in_=vec_all[:, 2 * H : 3 * H])
-                nc.vector.tensor_single_scalar(out=keep_f[:], in_=vec_all[:, H : 2 * H], scalar=P_KEEP, op=ALU.is_lt)
-                nc.vector.tensor_single_scalar(out=keep_bf[:], in_=vec_all[:, H : 2 * H], scalar=P_KEEP, op=ALU.is_lt)
             m = step - M_LAG
             if 0 <= m < n_runs:
                 index, start, n_rows = runs[m]
@@ -255,6 +261,13 @@ def tile_splitnn_pa_t_kernel(
                     accs[index] = psum_acc.tile([P, piece_rows, H], F32, name="acc")
                 codes, scales = quantised[m]
                 multiply_run(client, accs[index], start, n_rows, codes, scales)
+            if step == 2:
+                vec_all = psum_t.tile([P, 3 * H], F32, name="vec_all", tag="xt")
+                nc.tensor.matmul(out=vec_all[:], lhsT=ones_bf[:], rhs=vec_rows[:], start=True, stop=True)
+                nc.vector.tensor_copy(out=b1_f[:], in_=vec_all[:, 0:H])
+                nc.vector.tensor_copy(out=b2_f[:], in_=vec_all[:, 2 * H : 3 * H])
+                nc.vector.tensor_single_scalar(out=keep_f[:], in_=vec_all[:, H : 2 * H], scalar=P_KEEP, op=ALU.is_lt)
+                nc.vector.tensor_single_scalar(out=keep_bf[:], in_=vec_all[:, H : 2 * H], scalar=P_KEEP, op=ALU.is_lt)
             e = step - E_LAG
             if 0 <= e < n_runs:
                 index, start, n_rows = runs[e]

@@ -21,7 +21,7 @@ CHUNK = 4
 N_CHUNKS = ROWS // CHUNK
 Q_LAG, M_LAG, E_LAG = 1, 2, 3
 AHEAD = 4
-BY_ROW = 2
+BY_ROW = 3
 RUN = 4
 INV_EPS = 7.5
 P_KEEP = 0.95
@@ -58,6 +58,8 @@ def tile_splitnn_pa_t_kernel(
                 nc.scalar.dma_start(
                     out=vec_rows[0:1, i * H : (i + 1) * H], in_=vec.rearrange("(o h) -> o h", o=1)
                 )
+
+        load_vectors()
 
         ident = const.tile([P, P], F32, name="ident")
         make_identity(nc, ident[:])
@@ -96,11 +98,11 @@ def tile_splitnn_pa_t_kernel(
         def load_piece(index):
             client, first, n_rows = pieces[index]
             x_rows.append(load_x(client, first, n_rows, 1 if index < BY_ROW else n_rows))
-            if index == 1:
+            if index == 0:
                 load_weight(0, W1_words, W1_scales)
             if index == 4:
                 load_weight(1, W2_words, W2_scales)
-            late = index - 1
+            late = index - 2
             if 0 <= late < N_CHUNKS:
                 noise_sb = resident.tile([P, CHUNK, H], BF16, name="noise%d" % late)
                 nc.sync.dma_start(out=noise_sb[:], in_=noise_view[:, late * CHUNK : (late + 1) * CHUNK, :])
@@ -159,6 +161,14 @@ def tile_splitnn_pa_t_kernel(
         spread = const.tile([P, 2, P], F32, name="spread")
         tops = const.tile([P, 2], F32, name="tops")
         noise_mul = const.tile([P, 1], F32, name="noise_mul")
+
+        def spread_vectors():
+            vec_all = psum_t.tile([P, 3 * H], F32, name="vec_all", tag="xt")
+            nc.tensor.matmul(out=vec_all[:], lhsT=ones_bf[:], rhs=vec_rows[:], start=True, stop=True)
+            nc.vector.tensor_copy(out=b1_f[:], in_=vec_all[:, 0:H])
+            nc.vector.tensor_copy(out=b2_f[:], in_=vec_all[:, 2 * H : 3 * H])
+            nc.vector.tensor_single_scalar(out=keep_f[:], in_=vec_all[:, H : 2 * H], scalar=P_KEEP, op=ALU.is_lt)
+            nc.vector.tensor_single_scalar(out=keep_bf[:], in_=vec_all[:, H : 2 * H], scalar=P_KEEP, op=ALU.is_lt)
 
         def row_norms(a_sb, first):
             absolute = stage.tile([P, CHUNK, H], BF16, name="absolute")
@@ -243,7 +253,7 @@ def tile_splitnn_pa_t_kernel(
                 index, start, n_rows = runs[step]
                 grouped_of[step] = regroup_run(transpose_run(x_rows[index][start : start + n_rows]))
             if step == 0:
-                load_vectors()
+                spread_vectors()
             q = step - Q_LAG
             if 0 <= q < n_runs:
                 quantised[q] = quantise_run(grouped_of[q], runs[q][2])
@@ -261,13 +271,6 @@ def tile_splitnn_pa_t_kernel(
                     accs[index] = psum_acc.tile([P, piece_rows, H], F32, name="acc")
                 codes, scales = quantised[m]
                 multiply_run(client, accs[index], start, n_rows, codes, scales)
-            if step == 2:
-                vec_all = psum_t.tile([P, 3 * H], F32, name="vec_all", tag="xt")
-                nc.tensor.matmul(out=vec_all[:], lhsT=ones_bf[:], rhs=vec_rows[:], start=True, stop=True)
-                nc.vector.tensor_copy(out=b1_f[:], in_=vec_all[:, 0:H])
-                nc.vector.tensor_copy(out=b2_f[:], in_=vec_all[:, 2 * H : 3 * H])
-                nc.vector.tensor_single_scalar(out=keep_f[:], in_=vec_all[:, H : 2 * H], scalar=P_KEEP, op=ALU.is_lt)
-                nc.vector.tensor_single_scalar(out=keep_bf[:], in_=vec_all[:, H : 2 * H], scalar=P_KEEP, op=ALU.is_lt)
             e = step - E_LAG
             if 0 <= e < n_runs:
                 index, start, n_rows = runs[e]

@@ -19,10 +19,9 @@ PASSES = F // K_PASS
 ROWS = B // P
 CHUNK = 4
 N_CHUNKS = ROWS // CHUNK
-Q_LAG, M_LAG, E_LAG = 1, 2, 3
+Q_LAG, M_LAG = 1, 2
 AHEAD = 4
-BY_ROW = 3
-RUN = 4
+BY_ROW, BY_TWO = 2, 2
 INV_EPS = 7.5
 P_KEEP = 0.95
 
@@ -82,27 +81,27 @@ def tile_splitnn_pa_t_kernel(
                     in_=scale_rows[4 * quad : 4 * quad + 4],
                 )
 
-        def load_x(client, first, n_rows, rows_per_load):
-            row_words = []
-            for start in range(first, first + n_rows, rows_per_load):
-                x_sb = resident.tile([P, rows_per_load, F], BF16, name="x%d_%d" % (client, start))
-                nc.sync.dma_start(out=x_sb[:], in_=x_views[client][:, start : start + rows_per_load, :])
-                words = x_sb[:].bitcast(F32)
-                for i in range(rows_per_load):
-                    row_words.append(words[:, i, :])
-            return row_words
+        def load_x(client, start, n_rows):
+            x_sb = resident.tile([P, n_rows, F], BF16, name="x%d_%d" % (client, start))
+            nc.sync.dma_start(out=x_sb[:], in_=x_views[client][:, start : start + n_rows, :])
+            words = x_sb[:].bitcast(F32)
+            return [words[:, i, :] for i in range(n_rows)]
 
         x_rows = []
         noise = []
 
         def load_piece(index):
             client, first, n_rows = pieces[index]
-            x_rows.append(load_x(client, first, n_rows, 1 if index < BY_ROW else n_rows))
-            if index == 0:
-                load_weight(0, W1_words, W1_scales)
-            if index == 4:
+            rows_per_load = 1 if index < BY_ROW else 2 if index < BY_ROW + BY_TWO else n_rows
+            row_words = []
+            for start in range(0, n_rows, rows_per_load):
+                row_words += load_x(client, first + start, rows_per_load)
+                if index == 2 and start == 0:
+                    load_weight(0, W1_words, W1_scales)
+            x_rows.append(row_words)
+            if index == 6:
                 load_weight(1, W2_words, W2_scales)
-            late = index - 2
+            late = index - 3
             if 0 <= late < N_CHUNKS:
                 noise_sb = resident.tile([P, CHUNK, H], BF16, name="noise%d" % late)
                 nc.sync.dma_start(out=noise_sb[:], in_=noise_view[:, late * CHUNK : (late + 1) * CHUNK, :])
@@ -135,12 +134,16 @@ def tile_splitnn_pa_t_kernel(
             nc.vector.quantize_mx(out=codes[:].bitcast(FP8X4), scales=scales[:], in_=grouped[:])
             return codes, scales
 
-        def multiply_run(client, acc, start, n_rows, codes, scales):
+        def multiply_run(index):
+            client, first, n_rows = pieces[index]
+            codes, scales = quantised[index]
+            acc = psum_acc.tile([P, n_rows, H], F32, name="acc")
+            accs[index] = acc
             for j in range(n_rows):
                 for g in range(PASSES):
                     cols = slice((j * PASSES + g) * P, (j * PASSES + g + 1) * P)
                     nc.tensor.matmul_mx(
-                        out=acc[:, start + j, :],
+                        out=acc[:, j, :],
                         lhsT=codes[:, cols].bitcast(FP8X4),
                         lhsT_scale=scales[:, cols],
                         rhs=w_words[client][:, g, :].bitcast(FP4X4),
@@ -170,7 +173,15 @@ def tile_splitnn_pa_t_kernel(
             nc.vector.tensor_single_scalar(out=keep_f[:], in_=vec_all[:, H : 2 * H], scalar=P_KEEP, op=ALU.is_lt)
             nc.vector.tensor_single_scalar(out=keep_bf[:], in_=vec_all[:, H : 2 * H], scalar=P_KEEP, op=ALU.is_lt)
 
-        def row_norms(a_sb, first):
+        def add_bias(index):
+            client, first, n_rows = pieces[index]
+            biased = stage.tile([P, n_rows, H], F32, name="biased")
+            bias = b1_f if client == 0 else b2_f
+            nc.vector.tensor_tensor(out=biased[:], in0=accs[index][:], in1=over_rows(bias, n_rows), op=ALU.add)
+            biased_of[index] = biased
+
+        def row_norms(index):
+            a_sb, first = biased_of[index], pieces[index][1]
             absolute = stage.tile([P, CHUNK, H], BF16, name="absolute")
             for j in range(CHUNK):
                 nc.scalar.activation(
@@ -187,21 +198,13 @@ def tile_splitnn_pa_t_kernel(
 
         c_tiles = []
 
-        def mask_client0(chunk, a_sb):
+        def mask_client0(chunk):
             nc.vector.tensor_tensor(
                 out=noise[chunk][:], in0=noise[chunk][:], in1=over_rows(keep_bf, CHUNK), op=ALU.mult
             )
             c_sb = resident.tile([P, CHUNK, H], F32, name="c%d" % chunk)
             c_tiles.append(c_sb)
-            nc.vector.tensor_tensor(out=c_sb[:], in0=a_sb[:], in1=over_rows(keep_f, CHUNK), op=ALU.mult)
-
-        def finish_client0(index, acc):
-            first = pieces[index][1]
-            chunk = first // CHUNK
-            a_sb = stage.tile([P, CHUNK, H], F32, name="a_sb")
-            nc.vector.tensor_tensor(out=a_sb[:], in0=acc[:], in1=over_rows(b1_f, CHUNK), op=ALU.add)
-            norms_due.append((a_sb, first))
-            mask_client0(chunk, a_sb)
+            nc.vector.tensor_tensor(out=c_sb[:], in0=biased_of[chunk][:], in1=over_rows(keep_f, CHUNK), op=ALU.mult)
 
         def find_extremes():
             nc.vector.tensor_reduce(out=extremes[:, 0:1], in_=norms[:], axis=AXIS.X, op=ALU.max)
@@ -211,16 +214,23 @@ def tile_splitnn_pa_t_kernel(
                 out=spread[:, 1, :], in0=extremes[:, 1:2].to_broadcast([P, P]), scalar1=-1.0
             )
 
-        def finish_client1(index, acc):
+        def spread_extremes():
+            spread_t = psum_t.tile([P, 2, P], F32, name="spread_t", tag="xt")
+            spread_ts.append(spread_t)
+            for i in range(2):
+                nc.tensor.transpose(spread_t[:, i, :], spread[:, i, :], ident[:])
+
+        def find_noise_mul():
+            nc.vector.tensor_reduce(out=tops[:], in_=spread_ts[0][:], axis=AXIS.X, op=ALU.max)
+            nc.vector.tensor_scalar(
+                out=noise_mul[:], in0=tops[:, 0:1], scalar1=tops[:, 1:2], scalar2=INV_EPS,
+                op0=ALU.add, op1=ALU.mult,
+            )
+
+        def finish_client1(index):
             client, first, n_rows = pieces[index]
-            d_sb = stage.tile([P, n_rows, H], F32, name="d_sb")
-            nc.vector.tensor_tensor(out=d_sb[:], in0=acc[:], in1=over_rows(b2_f, n_rows), op=ALU.add)
+            d_sb = biased_of[index]
             if first == 0:
-                nc.vector.tensor_reduce(out=tops[:], in_=spread_ts[0][:], axis=AXIS.X, op=ALU.max)
-                nc.vector.tensor_scalar(
-                    out=noise_mul[:], in0=tops[:, 0:1], scalar1=tops[:, 1:2], scalar2=INV_EPS,
-                    op0=ALU.add, op1=ALU.mult,
-                )
                 add_noise(0)
             if first % CHUNK == 0 and first + CHUNK < ROWS:
                 add_noise(first // CHUNK + 1)
@@ -231,52 +241,40 @@ def tile_splitnn_pa_t_kernel(
             )
             nc.sync.dma_start(out=out_view[:, first : first + n_rows, :], in_=d_sb[:])
 
-        runs = []
-        for index, piece in enumerate(pieces):
-            for start in range(0, piece[2], RUN):
-                runs.append((index, start, min(RUN, piece[2] - start)))
-        n_runs = len(runs)
-
-        norms_due = []
         grouped_of = {}
         quantised = {}
         accs = {}
+        biased_of = {}
         spread_ts = []
-        last0 = max(i for i in range(n_runs) if pieces[runs[i][0]][0] == 0)
-        for step in range(n_runs + E_LAG):
-            for a_sb, first in norms_due:
-                row_norms(a_sb, first)
+        last0 = ROWS // CHUNK - 1
+
+        norms_due = []
+        for step in range(n_pieces + M_LAG + 1):
+            for k in norms_due:
+                row_norms(k)
             norms_due.clear()
             if step + AHEAD < n_pieces:
                 load_piece(step + AHEAD)
-            if step < n_runs:
-                index, start, n_rows = runs[step]
-                grouped_of[step] = regroup_run(transpose_run(x_rows[index][start : start + n_rows]))
+            if step < n_pieces:
+                grouped_of[step] = regroup_run(transpose_run(x_rows[step]))
             if step == 0:
                 spread_vectors()
             q = step - Q_LAG
-            if 0 <= q < n_runs:
-                quantised[q] = quantise_run(grouped_of[q], runs[q][2])
-            if step == last0 + E_LAG + 1:
+            if 0 <= q < n_pieces:
+                quantised[q] = quantise_run(grouped_of[q], pieces[q][2])
+            if step == last0 + M_LAG + 2:
                 find_extremes()
-                spread_t = psum_t.tile([P, 2, P], F32, name="spread_t", tag="xt")
-                spread_ts.append(spread_t)
-                for i in range(2):
-                    nc.tensor.transpose(spread_t[:, i, :], spread[:, i, :], ident[:])
+                spread_extremes()
             m = step - M_LAG
-            if 0 <= m < n_runs:
-                index, start, n_rows = runs[m]
-                client, first, piece_rows = pieces[index]
-                if start == 0:
-                    accs[index] = psum_acc.tile([P, piece_rows, H], F32, name="acc")
-                codes, scales = quantised[m]
-                multiply_run(client, accs[index], start, n_rows, codes, scales)
-            e = step - E_LAG
-            if 0 <= e < n_runs:
-                index, start, n_rows = runs[e]
-                client, first, piece_rows = pieces[index]
-                if start + n_rows == piece_rows:
-                    if client == 0:
-                        finish_client0(index, accs[index])
-                    else:
-                        finish_client1(index, accs[index])
+            if 0 <= m < n_pieces:
+                multiply_run(m)
+            e = step - M_LAG - 1
+            if 0 <= e < n_pieces:
+                add_bias(e)
+                if e <= last0:
+                    norms_due.append(e)
+                    mask_client0(e)
+                else:
+                    if e == last0 + 1:
+                        find_noise_mul()
+                    finish_client1(e)

@@ -257,8 +257,6 @@ def tile_splitnn_pa_t_kernel(
                 load_piece(step + AHEAD)
             if step < n_pieces:
                 grouped_of[step] = regroup_run(transpose_run(x_rows[step]))
-            if step == 0:
-                spread_vectors()
             q = step - Q_LAG
             if 0 <= q < n_pieces:
                 quantised[q] = quantise_run(grouped_of[q], pieces[q][2])
@@ -268,6 +266,8 @@ def tile_splitnn_pa_t_kernel(
             m = step - M_LAG
             if 0 <= m < n_pieces:
                 multiply_run(m)
+            if step == 1:
+                spread_vectors()
             e = step - M_LAG - 1
             if 0 <= e < n_pieces:
                 add_bias(e)

@@ -123,9 +123,9 @@ def tile_splitnn_pa_t_kernel(
         def regroup_run(banks):
             n_rows = len(banks)
             grouped = stage.tile([P, n_rows * PASSES * P * 4], BF16, name="grouped", align_bytes=64)
-            words = grouped[:].bitcast(F32).rearrange("p (j g t u) -> p j g t u", j=n_rows, g=PASSES, u=2)
+            words = grouped[:].bitcast(F32).rearrange("p (g j t u) -> p g j t u", j=n_rows, g=PASSES, u=2)
             for j in range(n_rows):
-                nc.scalar.copy(out=words[:, j], in_=banks[j][:].rearrange("p g u t -> p g t u"))
+                nc.scalar.copy(out=words[:, :, j], in_=banks[j][:].rearrange("p g u t -> p g t u"))
             return grouped
 
         def quantise_run(grouped, n_rows):
@@ -141,7 +141,7 @@ def tile_splitnn_pa_t_kernel(
             accs[index] = acc
             for j in range(n_rows):
                 for g in range(PASSES):
-                    cols = slice((j * PASSES + g) * P, (j * PASSES + g + 1) * P)
+                    cols = slice((g * n_rows + j) * P, (g * n_rows + j + 1) * P)
                     nc.tensor.matmul_mx(
                         out=acc[:, j, :],
                         lhsT=codes[:, cols].bitcast(FP8X4),
@@ -152,11 +152,48 @@ def tile_splitnn_pa_t_kernel(
                         stop=(g == PASSES - 1),
                     )
 
+        def is_flipped(index):
+            client, first, n_rows = pieces[index]
+            return client == 1 and n_rows == CHUNK and first // CHUNK % 2 == 0
+
+        def multiply_flipped(index):
+            n_rows = pieces[index][2]
+            codes, scales = quantised[index]
+            acc = psum_acc.tile([P, n_rows * P], F32, name="acc_flipped", tag="acc")
+            accs[index] = acc
+            for g in range(PASSES):
+                cols = slice(g * n_rows * P, (g + 1) * n_rows * P)
+                nc.tensor.matmul_mx(
+                    out=acc[:],
+                    lhsT=w_words[1][:, g, :].bitcast(FP4X4),
+                    lhsT_scale=w_planes[1][:, g, :],
+                    rhs=codes[:, cols].bitcast(FP8X4),
+                    rhs_scale=scales[:, cols],
+                    start=(g == 0),
+                    stop=(g == PASSES - 1),
+                )
+
+        def add_flipped_bias(index):
+            n_rows = pieces[index][2]
+            d_flipped = stage.tile([P, n_rows, P], F32, name="d_flipped")
+            nc.scalar.activation(
+                out=d_flipped[:].rearrange("p j t -> p (j t)"), in_=accs[index][:], func=ACT.Identity, bias=b2_col[:, 0:1]
+            )
+            biased_of[index] = d_flipped
+
+        def turn_back(index):
+            n_rows = pieces[index][2]
+            turned = psum_t.tile([P, n_rows, H], F32, name="turned", tag="xt")
+            for j in range(n_rows):
+                nc.tensor.transpose(turned[:, j, :], biased_of[index][:, j, :], ident[:])
+            turned_of[index] = turned
+
         def over_rows(vec, n_rows):
             return vec[:].unsqueeze(1).to_broadcast([P, n_rows, H])
 
         b1_f = const.tile([P, H], F32, name="b1_f")
         b2_f = const.tile([P, H], F32, name="b2_f")
+        b2_col = const.tile([P, 2], F32, name="b2_col")
         keep_f = const.tile([P, H], F32, name="keep_f")
         keep_bf = const.tile([P, H], BF16, name="keep_bf")
         norms = const.tile([P, ROWS], F32, name="norms")
@@ -166,8 +203,11 @@ def tile_splitnn_pa_t_kernel(
         noise_mul = const.tile([P, 1], F32, name="noise_mul")
 
         def spread_vectors():
-            vec_all = psum_t.tile([P, 3 * H], F32, name="vec_all", tag="xt")
+            vec_all = psum_acc.tile([P, 3 * H], F32, name="vec_all", tag="acc")
             nc.tensor.matmul(out=vec_all[:], lhsT=ones_bf[:], rhs=vec_rows[:], start=True, stop=True)
+            col_all = psum_acc.tile([P, 2], F32, name="col_all", tag="acc")
+            nc.tensor.matmul(out=col_all[:], lhsT=vec_rows[:, 2 * H : 3 * H], rhs=ones_bf[:, 0:2], start=True, stop=True)
+            nc.vector.tensor_copy(out=b2_col[:], in_=col_all[:])
             nc.vector.tensor_copy(out=b1_f[:], in_=vec_all[:, 0:H])
             nc.vector.tensor_copy(out=b2_f[:], in_=vec_all[:, 2 * H : 3 * H])
             nc.vector.tensor_single_scalar(out=keep_f[:], in_=vec_all[:, H : 2 * H], scalar=P_KEEP, op=ALU.is_lt)
@@ -229,14 +269,14 @@ def tile_splitnn_pa_t_kernel(
 
         def finish_client1(index):
             client, first, n_rows = pieces[index]
-            d_sb = biased_of[index]
-            if first == 0:
-                add_noise(0)
-            if first % CHUNK == 0 and first + CHUNK < ROWS:
-                add_noise(first // CHUNK + 1)
             offset = first % CHUNK
+            if index in turned_of:
+                d_sb = stage.tile([P, n_rows, H], F32, name="d_sb")
+                d = turned_of[index]
+            else:
+                d_sb = d = biased_of[index]
             nc.vector.tensor_tensor(
-                out=d_sb[:], in0=d_sb[:], in1=c_tiles[first // CHUNK][:, offset : offset + n_rows, :],
+                out=d_sb[:], in0=d[:], in1=c_tiles[first // CHUNK][:, offset : offset + n_rows, :],
                 op=ALU.min,
             )
             nc.sync.dma_start(out=out_view[:, first : first + n_rows, :], in_=d_sb[:])
@@ -245,6 +285,7 @@ def tile_splitnn_pa_t_kernel(
         quantised = {}
         accs = {}
         biased_of = {}
+        turned_of = {}
         spread_ts = []
         last0 = ROWS // CHUNK - 1
 
@@ -255,6 +296,9 @@ def tile_splitnn_pa_t_kernel(
             norms_due.clear()
             if step + AHEAD < n_pieces:
                 load_piece(step + AHEAD)
+            e = step - M_LAG - 1
+            if 0 <= e < n_pieces and is_flipped(e):
+                add_flipped_bias(e)
             if step < n_pieces:
                 grouped_of[step] = regroup_run(transpose_run(x_rows[step]))
             q = step - Q_LAG
@@ -263,18 +307,30 @@ def tile_splitnn_pa_t_kernel(
             if step == last0 + M_LAG + 2:
                 find_extremes()
                 spread_extremes()
+            if 0 <= e < n_pieces and is_flipped(e):
+                turn_back(e)
             m = step - M_LAG
             if 0 <= m < n_pieces:
-                multiply_run(m)
+                if is_flipped(m):
+                    multiply_flipped(m)
+                else:
+                    multiply_run(m)
             if step == 1:
                 spread_vectors()
-            e = step - M_LAG - 1
+            if e - 1 >= 0 and is_flipped(e - 1):
+                finish_client1(e - 1)
             if 0 <= e < n_pieces:
-                add_bias(e)
+                if not is_flipped(e):
+                    add_bias(e)
                 if e <= last0:
                     norms_due.append(e)
                     mask_client0(e)
                 else:
                     if e == last0 + 1:
                         find_noise_mul()
-                    finish_client1(e)
+                        add_noise(0)
+                    client, first, n_rows = pieces[e]
+                    if first % CHUNK == 0 and first + CHUNK < ROWS:
+                        add_noise(first // CHUNK + 1)
+                    if not is_flipped(e):
+                        finish_client1(e)

@@ -154,7 +154,7 @@ def tile_splitnn_pa_t_kernel(
 
         def is_flipped(index):
             client, first, n_rows = pieces[index]
-            return client == 1 and n_rows == CHUNK and first // CHUNK % 2 == 0
+            return client == 1 and n_rows == CHUNK
 
         def multiply_flipped(index):
             n_rows = pieces[index][2]
@@ -198,7 +198,6 @@ def tile_splitnn_pa_t_kernel(
         keep_bf = const.tile([P, H], BF16, name="keep_bf")
         norms = const.tile([P, ROWS], F32, name="norms")
         extremes = const.tile([P, 2], F32, name="extremes")
-        spread = const.tile([P, 2, P], F32, name="spread")
         tops = const.tile([P, 2], F32, name="tops")
         noise_mul = const.tile([P, 1], F32, name="noise_mul")
 
@@ -249,22 +248,19 @@ def tile_splitnn_pa_t_kernel(
         def find_extremes():
             nc.vector.tensor_reduce(out=extremes[:, 0:1], in_=norms[:], axis=AXIS.X, op=ALU.max)
             nc.vector.tensor_reduce(out=extremes[:, 1:2], in_=norms[:], axis=AXIS.X, op=ALU.min)
-            nc.vector.tensor_copy(out=spread[:, 0, :], in_=extremes[:, 0:1].to_broadcast([P, P]))
-            nc.vector.tensor_scalar_mul(
-                out=spread[:, 1, :], in0=extremes[:, 1:2].to_broadcast([P, P]), scalar1=-1.0
-            )
 
         def spread_extremes():
             spread_t = psum_t.tile([P, 2, P], F32, name="spread_t", tag="xt")
             spread_ts.append(spread_t)
             for i in range(2):
-                nc.tensor.transpose(spread_t[:, i, :], spread[:, i, :], ident[:])
+                nc.tensor.transpose(spread_t[:, i, :], extremes[:, i : i + 1].to_broadcast([P, P]), ident[:])
 
         def find_noise_mul():
-            nc.vector.tensor_reduce(out=tops[:], in_=spread_ts[0][:], axis=AXIS.X, op=ALU.max)
+            nc.vector.tensor_reduce(out=tops[:, 0:1], in_=spread_ts[0][:, 0, :], axis=AXIS.X, op=ALU.max)
+            nc.vector.tensor_reduce(out=tops[:, 1:2], in_=spread_ts[0][:, 1, :], axis=AXIS.X, op=ALU.min)
             nc.vector.tensor_scalar(
                 out=noise_mul[:], in0=tops[:, 0:1], scalar1=tops[:, 1:2], scalar2=INV_EPS,
-                op0=ALU.add, op1=ALU.mult,
+                op0=ALU.subtract, op1=ALU.mult,
             )
 
         def finish_client1(index):

@@ -20,6 +20,8 @@ ROWS = B // P
 CHUNK = 4
 N_CHUNKS = ROWS // CHUNK
 Q_LAG, M_LAG = 1, 2
+LATE_PIECES = 3
+SCALAR_NORMS = 2
 AHEAD = 4
 BY_ROW, BY_TWO = 2, 2
 INV_EPS = 7.5
@@ -101,7 +103,7 @@ def tile_splitnn_pa_t_kernel(
             x_rows.append(row_words)
             if index == 6:
                 load_weight(1, W2_words, W2_scales)
-            late = index - 3
+            late = index - 9
             if 0 <= late < N_CHUNKS:
                 noise_sb = resident.tile([P, CHUNK, H], BF16, name="noise%d" % late)
                 nc.sync.dma_start(out=noise_sb[:], in_=noise_view[:, late * CHUNK : (late + 1) * CHUNK, :])
@@ -221,8 +223,8 @@ def tile_splitnn_pa_t_kernel(
 
         def row_norms(index):
             a_sb, first = biased_of[index], pieces[index][1]
-            absolute = stage.tile([P, CHUNK, H], BF16, name="absolute")
-            for j in range(CHUNK):
+            absolute = stage.tile([P, SCALAR_NORMS, H], BF16, name="absolute")
+            for j in range(SCALAR_NORMS):
                 nc.scalar.activation(
                     out=absolute[:, j, :], in_=a_sb[:, j, :], func=ACT.Abs,
                     accum_out=norms[:, first + j : first + j + 1],
@@ -237,13 +239,22 @@ def tile_splitnn_pa_t_kernel(
 
         c_tiles = []
 
-        def mask_client0(chunk):
+        def mask_noise(chunk):
             nc.vector.tensor_tensor(
                 out=noise[chunk][:], in0=noise[chunk][:], in1=over_rows(keep_bf, CHUNK), op=ALU.mult
             )
+
+        def mask_client0(chunk):
             c_sb = resident.tile([P, CHUNK, H], F32, name="c%d" % chunk)
             c_tiles.append(c_sb)
             nc.vector.tensor_tensor(out=c_sb[:], in0=biased_of[chunk][:], in1=over_rows(keep_f, CHUNK), op=ALU.mult)
+
+        def vector_norms(index, start):
+            first = pieces[index][1]
+            nc.vector.tensor_reduce(
+                out=norms[:, first + start : first + CHUNK], in_=biased_of[index][:, start:CHUNK, :],
+                axis=AXIS.X, op=ALU.add, apply_absolute_value=True,
+            )
 
         def find_extremes():
             nc.vector.tensor_reduce(out=extremes[:, 0:1], in_=norms[:], axis=AXIS.X, op=ALU.max)
@@ -285,48 +296,66 @@ def tile_splitnn_pa_t_kernel(
         spread_ts = []
         last0 = ROWS // CHUNK - 1
 
+        def multiply_step(k):
+            return k + (M_LAG if k < n_pieces - LATE_PIECES else 1)
+
         norms_due = []
-        for step in range(n_pieces + M_LAG + 1):
+        turned_due = []
+        noise_step = 0
+        for step in range(n_pieces + 2):
             for k in norms_due:
                 row_norms(k)
             norms_due.clear()
             if step + AHEAD < n_pieces:
                 load_piece(step + AHEAD)
-            e = step - M_LAG - 1
-            if 0 <= e < n_pieces and is_flipped(e):
-                add_flipped_bias(e)
+            sums = [k for k in range(n_pieces) if multiply_step(k) + 1 == step]
+            for e in sums:
+                if is_flipped(e):
+                    add_flipped_bias(e)
+            if last0 in sums:
+                add_bias(last0)
+                vector_norms(last0, 0)
+                mask_client0(last0)
+                find_extremes()
             if step < n_pieces:
-                grouped_of[step] = regroup_run(transpose_run(x_rows[step]))
+                banks = transpose_run(x_rows[step])
+                if last0 in sums:
+                    spread_extremes()
+                grouped_of[step] = regroup_run(banks)
             q = step - Q_LAG
             if 0 <= q < n_pieces:
                 quantised[q] = quantise_run(grouped_of[q], pieces[q][2])
-            if step == last0 + M_LAG + 2:
-                find_extremes()
-                spread_extremes()
-            if 0 <= e < n_pieces and is_flipped(e):
-                turn_back(e)
-            m = step - M_LAG
-            if 0 <= m < n_pieces:
-                if is_flipped(m):
-                    multiply_flipped(m)
-                else:
-                    multiply_run(m)
+            if last0 in sums:
+                mask_noise(0)
+                find_noise_mul()
+                add_noise(0)
+                noise_step = step
+            chunk = step - noise_step
+            if noise_step > 0 and 0 < chunk < N_CHUNKS:
+                add_noise(chunk)
+            if noise_step > 0 and chunk + 1 < N_CHUNKS:
+                mask_noise(chunk + 1)
+            for e in sums:
+                if is_flipped(e):
+                    turn_back(e)
+            for m in range(n_pieces):
+                if multiply_step(m) == step:
+                    if is_flipped(m):
+                        multiply_flipped(m)
+                    else:
+                        multiply_run(m)
             if step == 1:
                 spread_vectors()
-            if e - 1 >= 0 and is_flipped(e - 1):
-                finish_client1(e - 1)
-            if 0 <= e < n_pieces:
-                if not is_flipped(e):
+            for e in turned_due:
+                finish_client1(e)
+            turned_due = [e for e in sums if is_flipped(e)]
+            for e in sums:
+                if not is_flipped(e) and e != last0:
                     add_bias(e)
-                if e <= last0:
+                if e < last0:
                     norms_due.append(e)
+                    vector_norms(e, SCALAR_NORMS)
                     mask_client0(e)
-                else:
-                    if e == last0 + 1:
-                        find_noise_mul()
-                        add_noise(0)
-                    client, first, n_rows = pieces[e]
-                    if first % CHUNK == 0 and first + CHUNK < ROWS:
-                        add_noise(first // CHUNK + 1)
+                elif e > last0:
                     if not is_flipped(e):
                         finish_client1(e)

@@ -20,10 +20,10 @@ ROWS = B // P
 CHUNK = 4
 N_CHUNKS = ROWS // CHUNK
 Q_LAG, M_LAG = 1, 2
-LATE_PIECES = 3
-SCALAR_NORMS = 2
+LATE_PIECES = 2
+SCALAR_NORMS = 3
 AHEAD = 4
-BY_ROW, BY_TWO = 2, 2
+BY_ROW, BY_TWO = 2, 13
 INV_EPS = 7.5
 P_KEEP = 0.95
 

import concourse.mybir as mybir
from concourse.masks import make_identity

F32 = mybir.dt.float32
BF16 = mybir.dt.bfloat16
U8 = mybir.dt.uint8
U32 = mybir.dt.uint32
I32 = mybir.dt.int32
FP8X4 = mybir.dt.float8_e4m3fn_x4
FP4X4 = mybir.dt.float4_e2m1fn_x4
ALU = mybir.AluOpType
ACT = mybir.ActivationFunctionType
AXIS = mybir.AxisListType

P = 128
B, F, H = 4096, 1024, 128
K_PASS = 4 * P
PASSES = F // K_PASS
ROWS = B // P
CHUNK = 4
N_CHUNKS = ROWS // CHUNK
Q_LAG, M_LAG = 1, 2
LATE_PIECES = 2
SCALAR_NORMS = 3
AHEAD = 4
BY_ROW, BY_TWO = 2, 13
INV_EPS = 7.5
P_KEEP = 0.95

FLOPS = 2 * 2 * B * F * H


def tile_splitnn_pa_t_kernel(
    tc, x1, x2, W1_words, W1_scales, b1, W2_words, W2_scales, b2, noise_std, rr_uniform, out
):
    nc = tc.nc
    x_views = [x.rearrange("(p r) k -> p r k", r=ROWS) for x in (x1, x2)]
    noise_view = noise_std.rearrange("(p r) h -> p r h", r=ROWS)
    out_view = out.rearrange("(p r) h -> p r h", r=ROWS)

    pieces = [(0, first, CHUNK) for first in range(0, ROWS, CHUNK)]
    pieces += [(1, first, CHUNK) for first in range(0, ROWS - CHUNK, CHUNK)]
    pieces += [(1, first, CHUNK // 2) for first in range(ROWS - CHUNK, ROWS, CHUNK // 2)]
    n_pieces = len(pieces)

    with tc.tile_pool(name="const", bufs=1) as const, tc.tile_pool(
        name="resident", bufs=1
    ) as resident, tc.tile_pool(name="stage", bufs=4) as stage, tc.psum_pool(
        name="psum_t", bufs=6
    ) as psum_t, tc.psum_pool(name="psum_acc", bufs=2) as psum_acc, tc.manual_schedule():

        vec_rows = const.tile([P, 3 * H], BF16, name="vec_rows")
        nc.vector.memset(vec_rows[:], 0.0)
        ones_bf = const.tile([P, P], BF16, name="ones_bf")
        nc.vector.memset(ones_bf[:], 1.0)

        def load_vectors():
            for i, vec in enumerate((b1, rr_uniform, b2)):
                nc.scalar.dma_start(
                    out=vec_rows[0:1, i * H : (i + 1) * H], in_=vec.rearrange("(o h) -> o h", o=1)
                )

        load_vectors()

        ident = const.tile([P, P], F32, name="ident")
        make_identity(nc, ident[:])
        warm = const.tile([P, 1], F32, name="warm")
        nc.scalar.activation(out=warm[:], in_=ident[:, 0:1], func=ACT.Abs)

        w_words = [const.tile([P, PASSES, 2 * H], U8, name="w_words%d" % w, align_bytes=64) for w in range(2)]
        w_planes = [const.tile([P, PASSES, H], U8, name="w_planes%d" % w, align_bytes=64) for w in range(2)]
        for w in range(2):
            nc.vector.memset(w_planes[w][:].bitcast(I32), 0)

        def load_weight(w, words, scales):
            nc.sync.dma_start(
                out=w_words[w][:].bitcast(I32), in_=words.bitcast(I32).rearrange("g p b -> p g b")
            )
            scale_rows = scales.bitcast(I32).rearrange("g q n -> q g n")
            for quad in range(4):
                nc.sync.dma_start(
                    out=w_planes[w][32 * quad : 32 * quad + 4].bitcast(I32),
                    in_=scale_rows[4 * quad : 4 * quad + 4],
                )

        def load_x(client, start, n_rows):
            x_sb = resident.tile([P, n_rows, F], BF16, name="x%d_%d" % (client, start))
            nc.sync.dma_start(out=x_sb[:], in_=x_views[client][:, start : start + n_rows, :])
            words = x_sb[:].bitcast(F32)
            return [words[:, i, :] for i in range(n_rows)]

        x_rows = []
        noise = []

        def load_piece(index):
            client, first, n_rows = pieces[index]
            rows_per_load = 1 if index < BY_ROW else 2 if index < BY_ROW + BY_TWO else n_rows
            row_words = []
            for start in range(0, n_rows, rows_per_load):
                row_words += load_x(client, first + start, rows_per_load)
                if index == 2 and start == 0:
                    load_weight(0, W1_words, W1_scales)
            x_rows.append(row_words)
            if index == 6:
                load_weight(1, W2_words, W2_scales)
            late = index - 9
            if 0 <= late < N_CHUNKS:
                noise_sb = resident.tile([P, CHUNK, H], BF16, name="noise%d" % late)
                nc.sync.dma_start(out=noise_sb[:], in_=noise_view[:, late * CHUNK : (late + 1) * CHUNK, :])
                noise.append(noise_sb)

        for index in range(AHEAD):
            load_piece(index)

        def transpose_run(rows):
            banks = []
            for i, row in enumerate(rows):
                xt = psum_t.tile([P, PASSES, 2, P], F32, name="xt")
                for g in range(PASSES):
                    for u in range(2):
                        nc.tensor.transpose(xt[:, g, u, :], row[:, 256 * g + u : 256 * (g + 1) : 2], ident[:])
                banks.append(xt)
            return banks

        def regroup_run(banks):
            n_rows = len(banks)
            grouped = stage.tile([P, n_rows * PASSES * P * 4], BF16, name="grouped", align_bytes=64)
            words = grouped[:].bitcast(F32).rearrange("p (g j t u) -> p g j t u", j=n_rows, g=PASSES, u=2)
            for j in range(n_rows):
                nc.scalar.copy(out=words[:, :, j], in_=banks[j][:].rearrange("p g u t -> p g t u"))
            return grouped

        def quantise_run(grouped, n_rows):
            codes = stage.tile([P, n_rows * PASSES * P], U32, name="codes", align_bytes=64)
            scales = stage.tile([P, n_rows * PASSES * P], U8, name="scales", align_bytes=64)
            nc.vector.quantize_mx(out=codes[:].bitcast(FP8X4), scales=scales[:], in_=grouped[:])
            return codes, scales

        def multiply_run(index):
            client, first, n_rows = pieces[index]
            codes, scales = quantised[index]
            acc = psum_acc.tile([P, n_rows, H], F32, name="acc")
            accs[index] = acc
            for j in range(n_rows):
                for g in range(PASSES):
                    cols = slice((g * n_rows + j) * P, (g * n_rows + j + 1) * P)
                    nc.tensor.matmul_mx(
                        out=acc[:, j, :],
                        lhsT=codes[:, cols].bitcast(FP8X4),
                        lhsT_scale=scales[:, cols],
                        rhs=w_words[client][:, g, :].bitcast(FP4X4),
                        rhs_scale=w_planes[client][:, g, :],
                        start=(g == 0),
                        stop=(g == PASSES - 1),
                    )

        def is_flipped(index):
            client, first, n_rows = pieces[index]
            return client == 1 and n_rows == CHUNK

        def multiply_flipped(index):
            n_rows = pieces[index][2]
            codes, scales = quantised[index]
            acc = psum_acc.tile([P, n_rows * P], F32, name="acc_flipped", tag="acc")
            accs[index] = acc
            for g in range(PASSES):
                cols = slice(g * n_rows * P, (g + 1) * n_rows * P)
                nc.tensor.matmul_mx(
                    out=acc[:],
                    lhsT=w_words[1][:, g, :].bitcast(FP4X4),
                    lhsT_scale=w_planes[1][:, g, :],
                    rhs=codes[:, cols].bitcast(FP8X4),
                    rhs_scale=scales[:, cols],
                    start=(g == 0),
                    stop=(g == PASSES - 1),
                )

        def add_flipped_bias(index):
            n_rows = pieces[index][2]
            d_flipped = stage.tile([P, n_rows, P], F32, name="d_flipped")
            nc.scalar.activation(
                out=d_flipped[:].rearrange("p j t -> p (j t)"), in_=accs[index][:], func=ACT.Identity, bias=b2_col[:, 0:1]
            )
            biased_of[index] = d_flipped

        def turn_back(index):
            n_rows = pieces[index][2]
            turned = psum_t.tile([P, n_rows, H], F32, name="turned", tag="xt")
            for j in range(n_rows):
                nc.tensor.transpose(turned[:, j, :], biased_of[index][:, j, :], ident[:])
            turned_of[index] = turned

        def over_rows(vec, n_rows):
            return vec[:].unsqueeze(1).to_broadcast([P, n_rows, H])

        b1_f = const.tile([P, H], F32, name="b1_f")
        b2_f = const.tile([P, H], F32, name="b2_f")
        b2_col = const.tile([P, 2], F32, name="b2_col")
        keep_f = const.tile([P, H], F32, name="keep_f")
        keep_bf = const.tile([P, H], BF16, name="keep_bf")
        norms = const.tile([P, ROWS], F32, name="norms")
        extremes = const.tile([P, 2], F32, name="extremes")
        tops = const.tile([P, 2], F32, name="tops")
        noise_mul = const.tile([P, 1], F32, name="noise_mul")

        def spread_vectors():
            vec_all = psum_acc.tile([P, 3 * H], F32, name="vec_all", tag="acc")
            nc.tensor.matmul(out=vec_all[:], lhsT=ones_bf[:], rhs=vec_rows[:], start=True, stop=True)
            col_all = psum_acc.tile([P, 2], F32, name="col_all", tag="acc")
            nc.tensor.matmul(out=col_all[:], lhsT=vec_rows[:, 2 * H : 3 * H], rhs=ones_bf[:, 0:2], start=True, stop=True)
            nc.vector.tensor_copy(out=b2_col[:], in_=col_all[:])
            nc.vector.tensor_copy(out=b1_f[:], in_=vec_all[:, 0:H])
            nc.vector.tensor_copy(out=b2_f[:], in_=vec_all[:, 2 * H : 3 * H])
            nc.vector.tensor_single_scalar(out=keep_f[:], in_=vec_all[:, H : 2 * H], scalar=P_KEEP, op=ALU.is_lt)
            nc.vector.tensor_single_scalar(out=keep_bf[:], in_=vec_all[:, H : 2 * H], scalar=P_KEEP, op=ALU.is_lt)

        def add_bias(index):
            client, first, n_rows = pieces[index]
            biased = stage.tile([P, n_rows, H], F32, name="biased")
            bias = b1_f if client == 0 else b2_f
            nc.vector.tensor_tensor(out=biased[:], in0=accs[index][:], in1=over_rows(bias, n_rows), op=ALU.add)
            biased_of[index] = biased

        def row_norms(index):
            a_sb, first = biased_of[index], pieces[index][1]
            absolute = stage.tile([P, SCALAR_NORMS, H], BF16, name="absolute")
            for j in range(SCALAR_NORMS):
                nc.scalar.activation(
                    out=absolute[:, j, :], in_=a_sb[:, j, :], func=ACT.Abs,
                    accum_out=norms[:, first + j : first + j + 1],
                )

        def add_noise(chunk):
            flat_c = c_tiles[chunk][:].rearrange("p j h -> p (j h)")
            nc.vector.scalar_tensor_tensor(
                out=flat_c, in0=noise[chunk][:].rearrange("p j h -> p (j h)"),
                scalar=noise_mul[:, 0:1], in1=flat_c, op0=ALU.mult, op1=ALU.add,
            )

        c_tiles = []

        def mask_noise(chunk):
            nc.vector.tensor_tensor(
                out=noise[chunk][:], in0=noise[chunk][:], in1=over_rows(keep_bf, CHUNK), op=ALU.mult
            )

        def mask_client0(chunk):
            c_sb = resident.tile([P, CHUNK, H], F32, name="c%d" % chunk)
            c_tiles.append(c_sb)
            nc.vector.tensor_tensor(out=c_sb[:], in0=biased_of[chunk][:], in1=over_rows(keep_f, CHUNK), op=ALU.mult)

        def vector_norms(index, start):
            first = pieces[index][1]
            nc.vector.tensor_reduce(
                out=norms[:, first + start : first + CHUNK], in_=biased_of[index][:, start:CHUNK, :],
                axis=AXIS.X, op=ALU.add, apply_absolute_value=True,
            )

        def find_extremes():
            nc.vector.tensor_reduce(out=extremes[:, 0:1], in_=norms[:], axis=AXIS.X, op=ALU.max)
            nc.vector.tensor_reduce(out=extremes[:, 1:2], in_=norms[:], axis=AXIS.X, op=ALU.min)

        def spread_extremes():
            spread_t = psum_t.tile([P, 2, P], F32, name="spread_t", tag="xt")
            spread_ts.append(spread_t)
            for i in range(2):
                nc.tensor.transpose(spread_t[:, i, :], extremes[:, i : i + 1].to_broadcast([P, P]), ident[:])

        def find_noise_mul():
            nc.vector.tensor_reduce(out=tops[:, 0:1], in_=spread_ts[0][:, 0, :], axis=AXIS.X, op=ALU.max)
            nc.vector.tensor_reduce(out=tops[:, 1:2], in_=spread_ts[0][:, 1, :], axis=AXIS.X, op=ALU.min)
            nc.vector.tensor_scalar(
                out=noise_mul[:], in0=tops[:, 0:1], scalar1=tops[:, 1:2], scalar2=INV_EPS,
                op0=ALU.subtract, op1=ALU.mult,
            )

        def finish_client1(index):
            client, first, n_rows = pieces[index]
            offset = first % CHUNK
            if index in turned_of:
                d_sb = stage.tile([P, n_rows, H], F32, name="d_sb")
                d = turned_of[index]
            else:
                d_sb = d = biased_of[index]
            nc.vector.tensor_tensor(
                out=d_sb[:], in0=d[:], in1=c_tiles[first // CHUNK][:, offset : offset + n_rows, :],
                op=ALU.min,
            )
            nc.sync.dma_start(out=out_view[:, first : first + n_rows, :], in_=d_sb[:])

        grouped_of = {}
        quantised = {}
        accs = {}
        biased_of = {}
        turned_of = {}
        spread_ts = []
        last0 = ROWS // CHUNK - 1

        def multiply_step(k):
            return k + (M_LAG if k < n_pieces - LATE_PIECES else 1)

        norms_due = []
        turned_due = []
        noise_step = 0
        for step in range(n_pieces + 2):
            for k in norms_due:
                row_norms(k)
            norms_due.clear()
            if step + AHEAD < n_pieces:
                load_piece(step + AHEAD)
            sums = [k for k in range(n_pieces) if multiply_step(k) + 1 == step]
            for e in sums:
                if is_flipped(e):
                    add_flipped_bias(e)
            if last0 in sums:
                add_bias(last0)
                vector_norms(last0, 0)
                mask_client0(last0)
                find_extremes()
            if step < n_pieces:
                banks = transpose_run(x_rows[step])
                if last0 in sums:
                    spread_extremes()
                grouped_of[step] = regroup_run(banks)
            q = step - Q_LAG
            if 0 <= q < n_pieces:
                quantised[q] = quantise_run(grouped_of[q], pieces[q][2])
            if last0 in sums:
                mask_noise(0)
                find_noise_mul()
                add_noise(0)
                noise_step = step
            chunk = step - noise_step
            if noise_step > 0 and 0 < chunk < N_CHUNKS:
                add_noise(chunk)
            if noise_step > 0 and chunk + 1 < N_CHUNKS:
                mask_noise(chunk + 1)
            for e in sums:
                if is_flipped(e):
                    turn_back(e)
            for m in range(n_pieces):
                if multiply_step(m) == step:
                    if is_flipped(m):
                        multiply_flipped(m)
                    else:
                        multiply_run(m)
            if step == 1:
                spread_vectors()
            for e in turned_due:
                finish_client1(e)
            turned_due = [e for e in sums if is_flipped(e)]
            for e in sums:
                if not is_flipped(e) and e != last0:
                    add_bias(e)
                if e < last0:
                    norms_due.append(e)
                    vector_norms(e, SCALAR_NORMS)
                    mask_client0(e)
                elif e > last0:
                    if not is_flipped(e):
                        finish_client1(e)
